import numpy as np
import ml_dtypes


def mxq(x, axis, fmt="e4m3"):
    dtype, down = {"e4m3": (ml_dtypes.float8_e4m3fn, 7), "e5m2": (ml_dtypes.float8_e5m2, 14)}[fmt]
    v = np.moveaxis(np.asarray(x, np.float32).astype(ml_dtypes.bfloat16).astype(np.float64), axis, -1)
    blocks = v.reshape(v.shape[:-1] + (-1, 32))
    amax = np.abs(blocks).max(-1, keepdims=True)
    byte = np.maximum(np.where(amax > 0, np.frexp(amax)[1] - 1 + 127, 0) - down, 1)
    scale = np.exp2(byte - 127.0)
    codes = (blocks / scale).astype(np.float32).astype(dtype).astype(np.float64)
    return np.moveaxis((codes * scale).reshape(v.shape), -1, axis)


WIDE = False


def mx_kscale(k):
    if not WIDE:
        return np.ones(k)
    levels = np.array([10, -10, 5, -5, 0])
    if k % 512:
        return np.exp2(np.random.permutation(np.resize(levels, k // 32))).repeat(32)
    a = np.empty((k // 512, 16))
    for p in range(k // 512):
        a[p, :8] = np.random.permutation(np.resize(levels, 8))
        for g in range(8):
            far = levels[np.abs(levels - a[p, g]) >= 10]
            a[p, g + 8] = far[np.random.randint(len(far))]
    return np.exp2(a.ravel()).repeat(32)


BF16 = ml_dtypes.bfloat16


def bf(x):
    return np.asarray(x, np.float32).astype(BF16)


def f64(x):
    return np.asarray(x).astype(np.float64)


E2M1 = np.array([0.0, 0.5, 1.0, 1.5, 2.0, 3.0, 4.0, 6.0, -0.0, -0.5, -1.0, -1.5, -2.0, -3.0, -4.0, -6.0])


def pack_weight(w, fmt):
    k, n = w.shape
    w = f64(bf(w)).reshape(k // 32, 32, n)
    amax = np.abs(w).max(1)
    if fmt == "e4m3":
        byte = np.frexp(amax)[1] - 1 + 127 - 7
    else:
        mant, ex = np.frexp(amax / 6.0)
        byte = np.where(mant > 0.5, ex, ex - 1) + 127
    byte = np.clip(np.where(amax > 0, byte, 1), 1, 254)
    scaled = (w * np.exp2(127.0 - byte)[:, None, :]).reshape(k, n).astype(np.float32)
    by_word = np.ascontiguousarray(scaled.reshape(k // 512, 128, 4, n).transpose(0, 1, 3, 2))
    if fmt == "e4m3":
        words = by_word.astype(ml_dtypes.float8_e4m3fn).view(np.uint8)
    else:
        c = by_word.astype(ml_dtypes.float4_e2m1fn).view(np.uint8) & 0xF
        words = c[..., 0::2] | (c[..., 1::2] << 4)
    return np.ascontiguousarray(words), np.ascontiguousarray(byte.astype(np.uint8).reshape(k // 512, 16, n))


def unpack_weight(words, scales, fmt):
    g, p, n, _ = words.shape
    if fmt == "e4m3":
        vals = np.ascontiguousarray(words).view(ml_dtypes.float8_e4m3fn).astype(np.float64)
    else:
        nib = np.empty((g, p, n, 4), np.uint8)
        nib[..., 0::2] = words & 0xF
        nib[..., 1::2] = words >> 4
        vals = E2M1[nib]
    vals = vals * np.repeat(np.exp2(scales.astype(np.float64) - 127.0), 8, axis=1)[..., None]
    return vals.transpose(0, 1, 3, 2).reshape(g * 512, n)
def pack4(w):
    words, scales = pack_weight(w, "e2m1")
    return words.reshape(words.shape[0], 128, -1), scales


def unpack4(words, scales):
    return unpack_weight(words.reshape(words.shape[0], 128, -1, 2), scales, "e2m1")


N, F, K, D, E = 512, 2048, 1536, 1024, 1024
SIG = 2.0
PS = 16.0


def draw0():
    t, sx = mx_kscale(K), mx_kscale(F)
    s = np.concatenate([sx, np.ones(E)])
    g = SIG * np.random.standard_normal((N, K))
    e = np.exp(g - g.max(-1, keepdims=True))
    w = e / e.sum(-1, keepdims=True) * (np.random.uniform(size=K) * PS)[None, :]
    att_prior = bf(w * t[None, :])
    dic_words, dic_scales = pack4(np.random.standard_normal((K, D)) / t[:, None])
    x = bf(np.random.standard_normal((N, F)) * sx[None, :])
    cs_w_words, cs_w_scales = pack4((np.random.standard_normal((K, F + E)) * (F + E) ** -0.5 / s[None, :]).T)
    return {"att_prior": att_prior,
            "dic_words": dic_words,
            "dic_scales": dic_scales,
            "x": x,
            "cs_w_words": cs_w_words,
            "cs_w_scales": cs_w_scales,
            "cs_b": bf(np.random.standard_normal(K) * 0.1)}


def core(att_prior, dic_words, dic_scales, x, cs_w_words, cs_w_scales, cs_b):
    z = mxq(f64(att_prior), 1, "e4m3") @ unpack4(dic_words, dic_scales)
    xz = np.concatenate([f64(x), z], axis=1)
    causal_logits = (mxq(xz, 1, "e4m3") @ unpack4(cs_w_words, cs_w_scales)) + f64(cs_b)
    return causal_logits, z


def e4m3fn_bytes(y):
    return np.clip(np.asarray(y, np.float64), -448.0, 448.0).astype(np.float32).astype(ml_dtypes.float8_e4m3fn).view(np.uint8)


def e4m3fn_values(b):
    return np.asarray(b, np.uint8).view(ml_dtypes.float8_e4m3fn).astype(np.float64)


def setup_inputs():
    d = draw0()
    x0 = np.asarray(d['x']).astype(np.float64)
    s = (np.max(np.abs(x0), axis=(0,), keepdims=True) / 448.0).astype(np.float32)
    out = {}
    for k, v in d.items():
        if k == 'x':
            out['x_bytes'] = e4m3fn_bytes(x0 / s.astype(np.float64))
            out['x_scale'] = s
        else:
            out[k] = v
    return out


def reference(att_prior, dic_words, dic_scales, x_bytes, x_scale, cs_w_words, cs_w_scales, cs_b):
    return core(att_prior, dic_words, dic_scales, e4m3fn_values(x_bytes) * x_scale.astype(np.float64), cs_w_words, cs_w_scales, cs_b)

@@ -1,0 +1,264 @@
+from contextlib import ExitStack
+
+import concourse.mybir as mybir
+from concourse.masks import make_identity
+
+F32 = mybir.dt.float32
+BF16 = mybir.dt.bfloat16
+I32 = mybir.dt.int32
+U32 = mybir.dt.uint32
+U8 = mybir.dt.uint8
+FP8 = mybir.dt.float8_e4m3fn
+FP8X4 = mybir.dt.float8_e4m3fn_x4
+FP4X4 = mybir.dt.float4_e2m1fn_x4
+MULT = mybir.AluOpType.mult
+ADD = mybir.AluOpType.add
+
+P = 128
+N, F, K, D, E = 512, 2048, 1536, 1024, 1024
+TILES = N // P
+BANK = 512
+GA = K // 512
+GX = F // 512
+GZ = E // 512
+GW = GX + GZ
+NZ = D // BANK
+NL = K // BANK
+
+FLOPS = 2 * N * K * D + 2 * N * (F + E) * K
+
+
+def tile_visualdeconfounder_pb_w4_kernel(
+    tc, att_prior, dic_words, dic_scales, x_bytes, x_scale, cs_w_words, cs_w_scales, cs_b, out_0, out_1
+):
+    nc = tc.nc
+    with ExitStack() as ctx:
+        keep = ctx.enter_context(tc.tile_pool(name="keep", bufs=1))
+        turn = ctx.enter_context(tc.psum_pool(name="turn", bufs=3))
+        acc = ctx.enter_context(tc.psum_pool(name="acc", bufs=5))
+
+        def new(name, shape, dtype):
+            return keep.tile(shape, dtype, name=name, align_bytes=64)
+
+        ctx.enter_context(tc.manual_schedule())
+
+        dic = new("dic", [P, GA, 2 * D], U8)
+        dic_s = new("dic_s", [P, GA, D], U8)
+        csw = new("csw", [P, GW, 2 * K], U8)
+        csw_s = new("csw_s", [P, GW, K], U8)
+        s_rows = new("s_rows", [P, P], F32)
+        s_col = new("s_col", [P, F // P], F32)
+        s_all = new("s_all", [P, F], F32)
+        b_row = new("b_row", [P, K], BF16)
+        ones = new("ones", [P, P], BF16)
+        bias = new("bias", [P, K], F32)
+        ident = new("ident", [P, P], F32)
+
+        att = [new("att%d" % m, [P, K], BF16) for m in range(TILES)]
+        xb = [new("xb%d" % m, [P, F], U8) for m in range(TILES)]
+        xv = [new("xv%d" % m, [P, F], BF16) for m in range(TILES)]
+        a_grp = [new("a_grp%d" % m, [P, GA, P, 4], BF16) for m in range(TILES)]
+        a_cod = [new("a_cod%d" % m, [P, GA, P], U32) for m in range(TILES)]
+        a_scl = [new("a_scl%d" % m, [P, GA, P], U8) for m in range(TILES)]
+        w_grp = [new("w_grp%d" % m, [P, GW, P, 4], BF16) for m in range(TILES)]
+        x_cod = [new("x_cod%d" % m, [P, GX, P], U32) for m in range(TILES)]
+        x_scl = [new("x_scl%d" % m, [P, GX, P], U8) for m in range(TILES)]
+        z_cod = [new("z_cod%d" % m, [P, GZ, P], U32) for m in range(TILES)]
+        z_scl = [new("z_scl%d" % m, [P, GZ, P], U8) for m in range(TILES)]
+        zb = [new("zb%d" % m, [P, E], BF16) for m in range(TILES)]
+        zf = [new("zf%d" % m, [P, E], F32) for m in range(TILES)]
+        lo = [new("lo%d" % m, [P, K], F32) for m in range(TILES)]
+
+        def rows(m):
+            return slice(m * P, (m + 1) * P)
+
+        nc.vector.memset(dic_s[:].rearrange("p g n -> p (g n)").bitcast(I32), 0)
+        nc.vector.memset(s_rows[:], 0.0)
+        nc.vector.memset(b_row[:], 0.0)
+        nc.vector.memset(ones[:], 1.0)
+        make_identity(nc, ident[:])
+        nc.gpsimd.memset(csw_s[:].rearrange("p g n -> p (g n)").bitcast(I32), 0)
+
+        nc.scalar.dma_start(out=att[0][:], in_=att_prior[rows(0), :])
+        for q in range(4):
+            nc.sync.dma_start(
+                out=dic_s[32 * q : 32 * q + 4, :, :].bitcast(I32),
+                in_=dic_scales[:, 4 * q : 4 * q + 4, :].rearrange("g q n -> q g n").bitcast(I32),
+            )
+        for g in range(GA):
+            nc.sync.dma_start(out=dic[:, g, :].bitcast(I32), in_=dic_words[g].bitcast(I32))
+        nc.sync.dma_start(out=s_rows[0 : F // P, :], in_=x_scale.rearrange("o (c p) -> (o c) p", p=P))
+        nc.sync.dma_start(out=att[1][:], in_=att_prior[rows(1), :])
+        nc.sync.dma_start(out=xb[0][:], in_=x_bytes[rows(0), :])
+        nc.sync.dma_start(out=att[2][:], in_=att_prior[rows(2), :])
+        nc.sync.dma_start(out=att[3][:], in_=att_prior[rows(3), :])
+        nc.sync.dma_start(out=xb[1][:], in_=x_bytes[rows(1), :])
+        nc.sync.dma_start(out=b_row[0:1, :], in_=cs_b.rearrange("(o k) -> o k", o=1))
+        for q in range(4):
+            nc.sync.dma_start(
+                out=csw_s[32 * q : 32 * q + 4, :, :].bitcast(I32),
+                in_=cs_w_scales[:, 4 * q : 4 * q + 4, :].rearrange("g q n -> q g n").bitcast(I32),
+            )
+        for g in range(GW):
+            nc.sync.dma_start(out=csw[:, g, :].bitcast(I32), in_=cs_w_words[g].bitcast(I32))
+            if g == 1:
+                nc.sync.dma_start(out=xb[2][:], in_=x_bytes[rows(2), :])
+            if g == 3:
+                nc.sync.dma_start(out=xb[3][:], in_=x_bytes[rows(3), :])
+
+        def turn_words(words, first, count, copy, grp, g0):
+            for b in range(0, count, 2):
+                n = min(2, count - b)
+                bank = turn.tile([P, 4, P], F32, name="turned")
+                for i in range(2 * n):
+                    nc.tensor.transpose(bank[:, i, :], first(words, b + i // 2, i % 2), ident[:])
+                copy(
+                    out=grp[:, g0 + b : g0 + b + n, :, :].bitcast(F32),
+                    in_=bank[:, 0 : 2 * n, :].rearrange("p (g u) r -> p g r u", u=2),
+                )
+
+        def every_second(words, g, u):
+            return words[:, 256 * g + u : 256 * (g + 1) : 2]
+
+        def halves(words, g, u):
+            return words[:, 256 * g + 128 * u : 256 * g + 128 * (u + 1)]
+
+        def quantize(cod, scl, c0, grp, g0, n):
+            nc.vector.quantize_mx(
+                out=cod[:, c0 : c0 + n, :].rearrange("p g r -> p (g r)").bitcast(FP8X4),
+                scales=scl[:, c0 : c0 + n, :].rearrange("p g r -> p (g r)"),
+                in_=grp[:, g0 : g0 + n, :, :].rearrange("p g r t -> p (g r t)"),
+            )
+
+        def a_turn(m):
+            turn_words(att[m][:].bitcast(F32), every_second, GA, nc.scalar.copy, a_grp[m], 0)
+
+        def a_quant(m):
+            quantize(a_cod[m], a_scl[m], 0, a_grp[m], 0, 2)
+            quantize(a_cod[m], a_scl[m], 2, a_grp[m], 2, 1)
+
+        def x_scale_all():
+            bank = turn.tile([P, 4, P], F32, name="turned")
+            nc.tensor.transpose(bank[:, 0, :], s_rows[:], ident[:])
+            nc.scalar.copy(out=s_col[:], in_=bank[:, 0, 0 : F // P])
+            for b in range(F // BANK):
+                bank = turn.tile([P, 4, P], F32, name="turned")
+                for i in range(4):
+                    c = 4 * b + i
+                    nc.tensor.transpose(bank[:, i, :], s_col[:, c : c + 1].to_broadcast([P, P]), ident[:])
+                nc.scalar.copy(
+                    out=s_all[:, BANK * b : BANK * (b + 1)], in_=bank[:].rearrange("p i r -> p (i r)")
+                )
+
+        def bias_all():
+            for n in range(NL):
+                bank = acc.tile([P, BANK], F32, name="sums")
+                nc.tensor.matmul(bank[:], lhsT=ones[:], rhs=b_row[:, BANK * n : BANK * (n + 1)], start=True, stop=True)
+                nc.scalar.copy(out=bias[:, BANK * n : BANK * (n + 1)], in_=bank[:])
+
+        def x_value(m):
+            nc.vector.tensor_tensor(out=xv[m][:], in0=xb[m][:].bitcast(FP8), in1=s_all[:], op=MULT)
+
+        def x_turn(m):
+            turn_words(xv[m][:].bitcast(F32), every_second, GX, nc.scalar.copy, w_grp[m], 0)
+
+        def x_quant(m):
+            quantize(x_cod[m], x_scl[m], 0, w_grp[m], 0, GX)
+
+        def z_product(m):
+            banks = []
+            for n in range(NZ):
+                bank = acc.tile([P, BANK], F32, name="sums")
+                banks.append(bank)
+            for g in range(GA):
+                for n in range(NZ):
+                    nc.tensor.matmul_mx(
+                        out=banks[n][:],
+                        lhsT=a_cod[m][:, g, :].bitcast(FP8X4),
+                        lhsT_scale=a_scl[m][:, g, :],
+                        rhs=dic[:, g, 2 * BANK * n : 2 * BANK * (n + 1)].bitcast(FP4X4),
+                        rhs_scale=dic_s[:, g, BANK * n : BANK * (n + 1)],
+                        start=(g == 0),
+                        stop=(g == GA - 1),
+                    )
+            for n in range(NZ):
+                nc.scalar.copy(
+                    out=zb[m][:, BANK * n : BANK * (n + 1)].rearrange("m (u p e) -> m u p e", u=2, e=2),
+                    in_=banks[n][:].rearrange("m (p u e) -> m u p e", u=2, e=2),
+                )
+            for n in range(NZ):
+                nc.vector.tensor_copy(out=zf[m][:, BANK * n : BANK * (n + 1)], in_=banks[n][:])
+            nc.sync.dma_start(out=out_1[rows(m), :], in_=zf[m][:])
+
+        def z_turn(m):
+            turn_words(zb[m][:].bitcast(F32), halves, GZ, nc.scalar.copy, w_grp[m], GX)
+
+        def z_quant(m):
+            quantize(z_cod[m], z_scl[m], 0, w_grp[m], GX, GZ)
+
+        def logits(m):
+            banks = []
+            for n in range(NL):
+                bank = acc.tile([P, BANK], F32, name="sums")
+                banks.append(bank)
+
+            def one(g, n):
+                cod, scl, c = (x_cod[m], x_scl[m], g) if g < GX else (z_cod[m], z_scl[m], g - GX)
+                nc.tensor.matmul_mx(
+                    out=banks[n][:],
+                    lhsT=cod[:, c, :].bitcast(FP8X4),
+                    lhsT_scale=scl[:, c, :],
+                    rhs=csw[:, g, 2 * BANK * n : 2 * BANK * (n + 1)].bitcast(FP4X4),
+                    rhs_scale=csw_s[:, g, BANK * n : BANK * (n + 1)],
+                    start=(g == 0),
+                    stop=(g == GW - 1),
+                )
+
+            for g in range(GX):
+                for n in range(NL):
+                    one(g, n)
+            for n in range(NL):
+                for g in range(GX, GW):
+                    one(g, n)
+                cols = slice(BANK * n, BANK * (n + 1))
+                nc.vector.tensor_tensor(out=lo[m][:, cols], in0=banks[n][:], in1=bias[:, cols], op=ADD)
+                nc.sync.dma_start(out=out_0[rows(m), cols], in_=lo[m][:, cols])
+
+        a_turn(0)
+        a_quant(0)
+        x_scale_all()
+        a_turn(1)
+        a_quant(1)
+        z_product(0)
+        x_value(0)
+        a_turn(2)
+        a_quant(2)
+        z_product(1)
+        x_turn(0)
+        z_turn(0)
+        x_value(1)
+        x_quant(0)
+        z_quant(0)
+        a_turn(3)
+        a_quant(3)
+        z_product(2)
+        bias_all()
+        x_turn(1)
+        z_turn(1)
+        x_value(2)
+        x_quant(1)
+        z_quant(1)
+        z_product(3)
+        logits(0)
+        x_turn(2)
+        z_turn(2)
+        x_value(3)
+        x_quant(2)
+        z_quant(2)
+        logits(1)
+        x_turn(3)
+        z_turn(3)
+        x_quant(3)
+        z_quant(3)
+        logits(2)
+        logits(3)

@@ -16,14 +16,16 @@ ADD = mybir.AluOpType.add
 
 P = 128
 N, F, K, D, E = 512, 2048, 1536, 1024, 1024
-TILES = N // P
+PASS = 512
 BANK = 512
-GA = K // 512
-GX = F // 512
-GZ = E // 512
+TILES = N // P
+GA = K // PASS
+GX = F // PASS
+GZ = E // PASS
 GW = GX + GZ
 NZ = D // BANK
 NL = K // BANK
+STEPS = 2 * TILES
 
 FLOPS = 2 * N * K * D + 2 * N * (F + E) * K
 
@@ -35,230 +37,224 @@ def tile_visualdeconfounder_pb_w4_kernel(
     with ExitStack() as ctx:
         keep = ctx.enter_context(tc.tile_pool(name="keep", bufs=1))
         turn = ctx.enter_context(tc.psum_pool(name="turn", bufs=3))
-        acc = ctx.enter_context(tc.psum_pool(name="acc", bufs=5))
+        sums = ctx.enter_context(tc.psum_pool(name="sums", bufs=5))
+        ctx.enter_context(tc.manual_schedule())
 
         def new(name, shape, dtype):
             return keep.tile(shape, dtype, name=name, align_bytes=64)
 
-        ctx.enter_context(tc.manual_schedule())
+        def each(name, shape, dtype):
+            return [new("%s%d" % (name, m), shape, dtype) for m in range(TILES)]
 
-        dic = new("dic", [P, GA, 2 * D], U8)
-        dic_s = new("dic_s", [P, GA, D], U8)
-        csw = new("csw", [P, GW, 2 * K], U8)
-        csw_s = new("csw_s", [P, GW, K], U8)
-        s_rows = new("s_rows", [P, P], F32)
-        s_col = new("s_col", [P, F // P], F32)
-        s_all = new("s_all", [P, F], F32)
-        b_row = new("b_row", [P, K], BF16)
-        ones = new("ones", [P, P], BF16)
-        bias = new("bias", [P, K], F32)
         ident = new("ident", [P, P], F32)
-
-        att = [new("att%d" % m, [P, K], BF16) for m in range(TILES)]
-        xb = [new("xb%d" % m, [P, F], U8) for m in range(TILES)]
-        xv = [new("xv%d" % m, [P, F], BF16) for m in range(TILES)]
-        a_grp = [new("a_grp%d" % m, [P, GA, P, 4], BF16) for m in range(TILES)]
-        a_cod = [new("a_cod%d" % m, [P, GA, P], U32) for m in range(TILES)]
-        a_scl = [new("a_scl%d" % m, [P, GA, P], U8) for m in range(TILES)]
-        w_grp = [new("w_grp%d" % m, [P, GW, P, 4], BF16) for m in range(TILES)]
-        x_cod = [new("x_cod%d" % m, [P, GX, P], U32) for m in range(TILES)]
-        x_scl = [new("x_scl%d" % m, [P, GX, P], U8) for m in range(TILES)]
-        z_cod = [new("z_cod%d" % m, [P, GZ, P], U32) for m in range(TILES)]
-        z_scl = [new("z_scl%d" % m, [P, GZ, P], U8) for m in range(TILES)]
-        zb = [new("zb%d" % m, [P, E], BF16) for m in range(TILES)]
-        zf = [new("zf%d" % m, [P, E], F32) for m in range(TILES)]
-        lo = [new("lo%d" % m, [P, K], F32) for m in range(TILES)]
+        dic = new("dic", [P, GA, 2 * D], U8)
+        dic_scl = new("dic_scl", [P, GA, D], U8)
+        csw = new("csw", [P, GW, 2 * K], U8)
+        csw_scl = new("csw_scl", [P, GW, K], U8)
+        x_scl = new("x_scl", [P, GX, 4], F32)
+        bias = new("bias", [P, K], BF16)
+        att = each("att", [P, K], BF16)
+        a_grp = each("a_grp", [P, GA, P, 4], BF16)
+        a_cod = each("a_cod", [P, GA, P], U32)
+        a_scl = each("a_scl", [P, GA, P], U8)
+        xb = each("xb", [P, F], U8)
+        xv = each("xv", [P, F], BF16)
+        xo = each("xo", [P, F], BF16)
+        zo = each("zo", [P, E], BF16)
+        zf = each("zf", [P, E], F32)
+        w_grp = each("w_grp", [P, GW, P, 4], BF16)
+        w_cod = each("w_cod", [P, GW, P], U32)
+        w_scl = each("w_scl", [P, GW, P], U8)
+        lo = each("lo", [P, K], F32)
 
         def rows(m):
             return slice(m * P, (m + 1) * P)
 
-        nc.vector.memset(dic_s[:].rearrange("p g n -> p (g n)").bitcast(I32), 0)
-        nc.vector.memset(s_rows[:], 0.0)
-        nc.vector.memset(b_row[:], 0.0)
-        nc.vector.memset(ones[:], 1.0)
         make_identity(nc, ident[:])
-        nc.gpsimd.memset(csw_s[:].rearrange("p g n -> p (g n)").bitcast(I32), 0)
+        for scl in (dic_scl, csw_scl):
+            nc.vector.memset(scl[:].rearrange("p g n -> p (g n)").bitcast(I32), 0)
 
-        nc.scalar.dma_start(out=att[0][:], in_=att_prior[rows(0), :])
-        for q in range(4):
-            nc.sync.dma_start(
-                out=dic_s[32 * q : 32 * q + 4, :, :].bitcast(I32),
-                in_=dic_scales[:, 4 * q : 4 * q + 4, :].rearrange("g q n -> q g n").bitcast(I32),
-            )
-        for g in range(GA):
-            nc.sync.dma_start(out=dic[:, g, :].bitcast(I32), in_=dic_words[g].bitcast(I32))
-        nc.sync.dma_start(out=s_rows[0 : F // P, :], in_=x_scale.rearrange("o (c p) -> (o c) p", p=P))
-        nc.sync.dma_start(out=att[1][:], in_=att_prior[rows(1), :])
-        nc.sync.dma_start(out=xb[0][:], in_=x_bytes[rows(0), :])
-        nc.sync.dma_start(out=att[2][:], in_=att_prior[rows(2), :])
-        nc.sync.dma_start(out=att[3][:], in_=att_prior[rows(3), :])
-        nc.sync.dma_start(out=xb[1][:], in_=x_bytes[rows(1), :])
-        nc.sync.dma_start(out=b_row[0:1, :], in_=cs_b.rearrange("(o k) -> o k", o=1))
-        for q in range(4):
-            nc.sync.dma_start(
-                out=csw_s[32 * q : 32 * q + 4, :, :].bitcast(I32),
-                in_=cs_w_scales[:, 4 * q : 4 * q + 4, :].rearrange("g q n -> q g n").bitcast(I32),
-            )
-        for g in range(GW):
-            nc.sync.dma_start(out=csw[:, g, :].bitcast(I32), in_=cs_w_words[g].bitcast(I32))
-            if g == 1:
-                nc.sync.dma_start(out=xb[2][:], in_=x_bytes[rows(2), :])
-            if g == 3:
-                nc.sync.dma_start(out=xb[3][:], in_=x_bytes[rows(3), :])
+        def load_att(q, m, g0, g1):
+            cols = slice(PASS * g0, PASS * g1)
+            q.dma_start(out=att[m][:, cols], in_=att_prior[rows(m), cols])
 
-        def turn_words(words, first, count, copy, grp, g0):
-            for b in range(0, count, 2):
-                n = min(2, count - b)
-                bank = turn.tile([P, 4, P], F32, name="turned")
-                for i in range(2 * n):
-                    nc.tensor.transpose(bank[:, i, :], first(words, b + i // 2, i % 2), ident[:])
-                copy(
-                    out=grp[:, g0 + b : g0 + b + n, :, :].bitcast(F32),
-                    in_=bank[:, 0 : 2 * n, :].rearrange("p (g u) r -> p g r u", u=2),
+        def load_x(m):
+            nc.sync.dma_start(out=xb[m][:], in_=x_bytes[rows(m), :])
+
+        def load_words(tile, words, g):
+            nc.sync.dma_start(out=tile[:, g, :].bitcast(I32), in_=words[g].bitcast(I32))
+
+        def load_scales(tile, scales):
+            for q in range(4):
+                nc.sync.dma_start(
+                    out=tile[32 * q : 32 * q + 4, :, :].bitcast(I32),
+                    in_=scales[:, 4 * q : 4 * q + 4, :].rearrange("g q n -> q g n").bitcast(I32),
                 )
 
-        def every_second(words, g, u):
-            return words[:, 256 * g + u : 256 * (g + 1) : 2]
+        load_att(nc.scalar, 0, 0, 1)
+        load_att(nc.scalar, 0, 1, GA)
+        load_scales(dic_scl, dic_scales)
+        load_att(nc.sync, 1, 0, GA)
+        for g in range(GA):
+            load_words(dic, dic_words, g)
+        load_att(nc.sync, 2, 0, GA)
+        load_x(0)
+        nc.sync.dma_start(out=x_scl[:], in_=x_scale.rearrange("o (g p t) -> p (o g) t", p=P, t=4))
+        load_att(nc.sync, 3, 0, GA)
+        load_x(1)
+        for g in range(GX):
+            load_words(csw, cs_w_words, g)
+        load_scales(csw_scl, cs_w_scales)
+        load_x(2)
+        for g in range(GX, GW):
+            load_words(csw, cs_w_words, g)
+        load_x(3)
+        nc.sync.dma_start(out=bias[:], in_=cs_b.partition_broadcast(P))
 
-        def halves(words, g, u):
-            return words[:, 256 * g + 128 * u : 256 * g + 128 * (u + 1)]
+        def turned(src, pieces):
+            bank = turn.tile([P, 4, P], F32, name="turned")
+            words = src[:].bitcast(F32)
+            for i in range(len(pieces)):
+                nc.tensor.transpose(bank[:, i, :], words[:, pieces[i]], ident[:])
+            return bank
 
-        def quantize(cod, scl, c0, grp, g0, n):
+        def every_second(g0, n):
+            return [slice(256 * g + u, 256 * (g + 1), 2) for g in range(g0, g0 + n) for u in range(2)]
+
+        def side_by_side(g0, n):
+            return [slice(128 * i, 128 * (i + 1)) for i in range(2 * g0, 2 * (g0 + n))]
+
+        def emptied(bank, grp, g0, n):
+            nc.scalar.copy(
+                out=grp[:, g0 : g0 + n, :, :].bitcast(F32),
+                in_=bank[:, 0 : 2 * n, :].rearrange("p (g u) r -> p g r u", u=2),
+            )
+
+        def quantize(cod, scl, grp, g0, n):
             nc.vector.quantize_mx(
-                out=cod[:, c0 : c0 + n, :].rearrange("p g r -> p (g r)").bitcast(FP8X4),
-                scales=scl[:, c0 : c0 + n, :].rearrange("p g r -> p (g r)"),
+                out=cod[:, g0 : g0 + n, :].rearrange("p g r -> p (g r)").bitcast(FP8X4),
+                scales=scl[:, g0 : g0 + n, :].rearrange("p g r -> p (g r)"),
                 in_=grp[:, g0 : g0 + n, :, :].rearrange("p g r t -> p (g r t)"),
             )
 
-        def a_turn(m):
-            turn_words(att[m][:].bitcast(F32), every_second, GA, nc.scalar.copy, a_grp[m], 0)
+        def mx(bank, cod, scl, g, tile, tile_scl, gw, n, first, last):
+            nc.tensor.matmul_mx(
+                out=bank[:],
+                lhsT=cod[:, g, :].bitcast(FP8X4),
+                lhsT_scale=scl[:, g, :],
+                rhs=tile[:, gw, 2 * BANK * n : 2 * BANK * (n + 1)].bitcast(FP4X4),
+                rhs_scale=tile_scl[:, gw, BANK * n : BANK * (n + 1)],
+                start=first,
+                stop=last,
+            )
 
-        def a_quant(m):
-            quantize(a_cod[m], a_scl[m], 0, a_grp[m], 0, 2)
-            quantize(a_cod[m], a_scl[m], 2, a_grp[m], 2, 1)
-
-        def x_scale_all():
-            bank = turn.tile([P, 4, P], F32, name="turned")
-            nc.tensor.transpose(bank[:, 0, :], s_rows[:], ident[:])
-            nc.scalar.copy(out=s_col[:], in_=bank[:, 0, 0 : F // P])
-            for b in range(F // BANK):
-                bank = turn.tile([P, 4, P], F32, name="turned")
-                for i in range(4):
-                    c = 4 * b + i
-                    nc.tensor.transpose(bank[:, i, :], s_col[:, c : c + 1].to_broadcast([P, P]), ident[:])
-                nc.scalar.copy(
-                    out=s_all[:, BANK * b : BANK * (b + 1)], in_=bank[:].rearrange("p i r -> p (i r)")
-                )
-
-        def bias_all():
-            for n in range(NL):
-                bank = acc.tile([P, BANK], F32, name="sums")
-                nc.tensor.matmul(bank[:], lhsT=ones[:], rhs=b_row[:, BANK * n : BANK * (n + 1)], start=True, stop=True)
-                nc.scalar.copy(out=bias[:, BANK * n : BANK * (n + 1)], in_=bank[:])
-
-        def x_value(m):
-            nc.vector.tensor_tensor(out=xv[m][:], in0=xb[m][:].bitcast(FP8), in1=s_all[:], op=MULT)
-
-        def x_turn(m):
-            turn_words(xv[m][:].bitcast(F32), every_second, GX, nc.scalar.copy, w_grp[m], 0)
-
-        def x_quant(m):
-            quantize(x_cod[m], x_scl[m], 0, w_grp[m], 0, GX)
-
-        def z_product(m):
+        def sum_banks(count):
             banks = []
-            for n in range(NZ):
-                bank = acc.tile([P, BANK], F32, name="sums")
+            for n in range(count):
+                bank = sums.tile([P, BANK], F32, name="sum")
                 banks.append(bank)
-            for g in range(GA):
+            return banks
+
+        def x_widen(m, h):
+            cols = slice(1024 * h, 1024 * (h + 1))
+            COPYX = nc.vector.tensor_copy if m < 2 else nc.scalar.copy
+            COPYX(out=xv[m][:, cols], in_=xb[m][:, cols].bitcast(FP8))
+
+        def x_order(m, h):
+            cols = slice(1024 * h, 1024 * (h + 1))
+            nc.vector.tensor_copy(
+                out=xo[m][:, cols].bitcast(F32).rearrange("r (g u p) -> r g u p", u=2, p=P),
+                in_=xv[m][:, cols].bitcast(F32).rearrange("r (g p u) -> r g u p", u=2, p=P),
+            )
+
+        def x_scaled(bank, m, h, i):
+            g = 2 * h + i
+            nc.vector.tensor_tensor(
+                out=w_grp[m][:, g, :, :].rearrange("p r (u e) -> p r u e", u=2),
+                in0=bank[:, 2 * i : 2 * i + 2, :].bitcast(BF16).rearrange("p u (r e) -> p r u e", e=2),
+                in1=x_scl[:, g, :].rearrange("p (o u e) -> p o u e", o=1, u=2).to_broadcast([P, P, 2, 2]),
+                op=MULT,
+            )
+
+        def z_round(bank, m, n):
+            nc.scalar.copy(
+                out=zo[m][:, BANK * n : BANK * (n + 1)].rearrange("r (u p e) -> r u p e", u=2, e=2),
+                in_=bank[:].rearrange("r (p u e) -> r u p e", u=2, e=2),
+            )
+
+        def z_keep(bank, m, n):
+            nc.scalar.copy(out=zf[m][:, BANK * n : BANK * (n + 1)], in_=bank[:])
+
+
+        def a_stage(m, cuts):
+            for g0, n in cuts:
+                bank = turned(att[m], every_second(g0, n))
+                emptied(bank, a_grp[m], g0, n)
+
+        def a_quant(m, cuts):
+            for g0, n in cuts:
+                quantize(a_cod[m], a_scl[m], a_grp[m], g0, n)
+
+        FIRST = [(0, 1), (1, 2)]
+        CUTS = [(0, 2), (2, 1)]
+        a_stage(0, FIRST)
+        a_quant(0, FIRST)
+        a_stage(1, CUTS)
+        a_quant(1, CUTS)
+
+        for step in range(STEPS):
+            a, x, z, l = step + 2, step - 2, step - 1, step - TILES
+            xn = {0: [(0, 0), (0, 1)], 1: [(1, 0), (1, 1)], 2: [], 3: [(2, 0), (2, 1)], 4: [(3, 0), (3, 1)]}.get(step, [])
+            if step < TILES:
+                zbanks = sum_banks(NZ)
+                for g in range(GA):
+                    for n in range(NZ):
+                        mx(zbanks[n], a_cod[step], a_scl[step], g, dic, dic_scl, g, n, g == 0, g == GA - 1)
                 for n in range(NZ):
-                    nc.tensor.matmul_mx(
-                        out=banks[n][:],
-                        lhsT=a_cod[m][:, g, :].bitcast(FP8X4),
-                        lhsT_scale=a_scl[m][:, g, :],
-                        rhs=dic[:, g, 2 * BANK * n : 2 * BANK * (n + 1)].bitcast(FP4X4),
-                        rhs_scale=dic_s[:, g, BANK * n : BANK * (n + 1)],
-                        start=(g == 0),
-                        stop=(g == GA - 1),
-                    )
-            for n in range(NZ):
-                nc.scalar.copy(
-                    out=zb[m][:, BANK * n : BANK * (n + 1)].rearrange("m (u p e) -> m u p e", u=2, e=2),
-                    in_=banks[n][:].rearrange("m (p u e) -> m u p e", u=2, e=2),
-                )
-            for n in range(NZ):
-                nc.vector.tensor_copy(out=zf[m][:, BANK * n : BANK * (n + 1)], in_=banks[n][:])
-            nc.sync.dma_start(out=out_1[rows(m), :], in_=zf[m][:])
-
-        def z_turn(m):
-            turn_words(zb[m][:].bitcast(F32), halves, GZ, nc.scalar.copy, w_grp[m], GX)
-
-        def z_quant(m):
-            quantize(z_cod[m], z_scl[m], 0, w_grp[m], GX, GZ)
-
-        def logits(m):
-            banks = []
-            for n in range(NL):
-                bank = acc.tile([P, BANK], F32, name="sums")
-                banks.append(bank)
-
-            def one(g, n):
-                cod, scl, c = (x_cod[m], x_scl[m], g) if g < GX else (z_cod[m], z_scl[m], g - GX)
-                nc.tensor.matmul_mx(
-                    out=banks[n][:],
-                    lhsT=cod[:, c, :].bitcast(FP8X4),
-                    lhsT_scale=scl[:, c, :],
-                    rhs=csw[:, g, 2 * BANK * n : 2 * BANK * (n + 1)].bitcast(FP4X4),
-                    rhs_scale=csw_s[:, g, BANK * n : BANK * (n + 1)],
-                    start=(g == 0),
-                    stop=(g == GW - 1),
-                )
-
-            for g in range(GX):
+                    z_round(zbanks[n], step, n)
+                nc.vector.tensor_copy(out=zf[step][:, 0:BANK], in_=zbanks[0][:])
+            elif l < TILES - 1:
+                lbanks = sum_banks(NL)
+                for g in range(GX):
+                    for n in range(NL):
+                        mx(lbanks[n], w_cod[l], w_scl[l], g, csw, csw_scl, g, n, g == 0, False)
                 for n in range(NL):
-                    one(g, n)
-            for n in range(NL):
-                for g in range(GX, GW):
-                    one(g, n)
-                cols = slice(BANK * n, BANK * (n + 1))
-                nc.vector.tensor_tensor(out=lo[m][:, cols], in0=banks[n][:], in1=bias[:, cols], op=ADD)
-                nc.sync.dma_start(out=out_0[rows(m), cols], in_=lo[m][:, cols])
-
-        a_turn(0)
-        a_quant(0)
-        x_scale_all()
-        a_turn(1)
-        a_quant(1)
-        z_product(0)
-        x_value(0)
-        a_turn(2)
-        a_quant(2)
-        z_product(1)
-        x_turn(0)
-        z_turn(0)
-        x_value(1)
-        x_quant(0)
-        z_quant(0)
-        a_turn(3)
-        a_quant(3)
-        z_product(2)
-        bias_all()
-        x_turn(1)
-        z_turn(1)
-        x_value(2)
-        x_quant(1)
-        z_quant(1)
-        z_product(3)
-        logits(0)
-        x_turn(2)
-        z_turn(2)
-        x_value(3)
-        x_quant(2)
-        z_quant(2)
-        logits(1)
-        x_turn(3)
-        z_turn(3)
-        x_quant(3)
-        z_quant(3)
-        logits(2)
-        logits(3)
+                    for g in range(GX, GW):
+                        mx(lbanks[n], w_cod[l], w_scl[l], g, csw, csw_scl, g, n, False, g == GW - 1)
+            else:
+                lbanks = sum_banks(NL)
+                for n in range(NL):
+                    for g in range(GW):
+                        mx(lbanks[n], w_cod[l], w_scl[l], g, csw, csw_scl, g, n, g == 0, g == GW - 1)
+            for m, h in xn:
+                x_widen(m, h)
+            if a < TILES:
+                a_stage(a, CUTS)
+            if 0 <= x < TILES:
+                xbanks = [turned(xo[x], side_by_side(2 * h, 2)) for h in range(2)]
+            if 0 <= z < TILES:
+                bank = turned(zo[z], side_by_side(0, 2))
+            if step < TILES:
+                z_keep(zbanks[1], step, 1)
+                nc.sync.dma_start(out=out_1[rows(step), :], in_=zf[step][:])
+            if 0 <= z < TILES:
+                emptied(bank, w_grp[z], GX, GZ)
+            for m, h in xn:
+                x_order(m, h)
+            if a < TILES:
+                a_quant(a, CUTS)
+            if step >= TILES:
+                for n in range(NL):
+                    parts = 2 if step == STEPS - 1 and n == NL - 1 else 1
+                    for i in range(parts):
+                        w = BANK // parts
+                        cols = slice(BANK * n + w * i, BANK * n + w * (i + 1))
+                        nc.vector.tensor_tensor(out=lo[l][:, cols], in0=lbanks[n][:, w * i : w * (i + 1)], in1=bias[:, cols], op=ADD)
+                        nc.sync.dma_start(out=out_0[rows(l), cols], in_=lo[l][:, cols])
+            if 0 <= x < TILES:
+                for h in range(2):
+                    for i in range(2):
+                        x_scaled(xbanks[h], x, h, i)
+                quantize(w_cod[x], w_scl[x], w_grp[x], 0, GX)
+            if 0 <= z < TILES:
+                quantize(w_cod[z], w_scl[z], w_grp[z], GX, GZ)

from contextlib import ExitStack

import concourse.mybir as mybir
from concourse.masks import make_identity

F32 = mybir.dt.float32
BF16 = mybir.dt.bfloat16
I32 = mybir.dt.int32
U32 = mybir.dt.uint32
U8 = mybir.dt.uint8
FP8 = mybir.dt.float8_e4m3fn
FP8X4 = mybir.dt.float8_e4m3fn_x4
FP4X4 = mybir.dt.float4_e2m1fn_x4
MULT = mybir.AluOpType.mult
ADD = mybir.AluOpType.add

P = 128
N, F, K, D, E = 512, 2048, 1536, 1024, 1024
PASS = 512
BANK = 512
TILES = N // P
GA = K // PASS
GX = F // PASS
GZ = E // PASS
GW = GX + GZ
NZ = D // BANK
NL = K // BANK
STEPS = 2 * TILES

FLOPS = 2 * N * K * D + 2 * N * (F + E) * K


def tile_visualdeconfounder_pb_w4_kernel(
    tc, att_prior, dic_words, dic_scales, x_bytes, x_scale, cs_w_words, cs_w_scales, cs_b, out_0, out_1
):
    nc = tc.nc
    with ExitStack() as ctx:
        keep = ctx.enter_context(tc.tile_pool(name="keep", bufs=1))
        turn = ctx.enter_context(tc.psum_pool(name="turn", bufs=3))
        sums = ctx.enter_context(tc.psum_pool(name="sums", bufs=5))
        ctx.enter_context(tc.manual_schedule())

        def new(name, shape, dtype):
            return keep.tile(shape, dtype, name=name, align_bytes=64)

        def each(name, shape, dtype):
            return [new("%s%d" % (name, m), shape, dtype) for m in range(TILES)]

        ident = new("ident", [P, P], F32)
        dic = new("dic", [P, GA, 2 * D], U8)
        dic_scl = new("dic_scl", [P, GA, D], U8)
        csw = new("csw", [P, GW, 2 * K], U8)
        csw_scl = new("csw_scl", [P, GW, K], U8)
        x_scl = new("x_scl", [P, GX, 4], F32)
        bias = new("bias", [P, K], BF16)
        att = each("att", [P, K], BF16)
        a_grp = each("a_grp", [P, GA, P, 4], BF16)
        a_cod = each("a_cod", [P, GA, P], U32)
        a_scl = each("a_scl", [P, GA, P], U8)
        xb = each("xb", [P, F], U8)
        xv = each("xv", [P, F], BF16)
        xo = each("xo", [P, F], BF16)
        zo = each("zo", [P, E], BF16)
        zf = each("zf", [P, E], F32)
        w_grp = each("w_grp", [P, GW, P, 4], BF16)
        w_cod = each("w_cod", [P, GW, P], U32)
        w_scl = each("w_scl", [P, GW, P], U8)
        lo = each("lo", [P, K], F32)

        def rows(m):
            return slice(m * P, (m + 1) * P)

        make_identity(nc, ident[:])
        for scl in (dic_scl, csw_scl):
            nc.vector.memset(scl[:].rearrange("p g n -> p (g n)").bitcast(I32), 0)

        def load_att(q, m, g0, g1):
            cols = slice(PASS * g0, PASS * g1)
            q.dma_start(out=att[m][:, cols], in_=att_prior[rows(m), cols])

        def load_x(m):
            nc.sync.dma_start(out=xb[m][:], in_=x_bytes[rows(m), :])

        def load_words(tile, words, g):
            nc.sync.dma_start(out=tile[:, g, :].bitcast(I32), in_=words[g].bitcast(I32))

        def load_scales(tile, scales):
            for q in range(4):
                nc.sync.dma_start(
                    out=tile[32 * q : 32 * q + 4, :, :].bitcast(I32),
                    in_=scales[:, 4 * q : 4 * q + 4, :].rearrange("g q n -> q g n").bitcast(I32),
                )

        load_att(nc.scalar, 0, 0, 1)
        load_att(nc.scalar, 0, 1, GA)
        load_scales(dic_scl, dic_scales)
        load_att(nc.sync, 1, 0, GA)
        for g in range(GA):
            load_words(dic, dic_words, g)
        load_att(nc.sync, 2, 0, GA)
        load_x(0)
        nc.sync.dma_start(out=x_scl[:], in_=x_scale.rearrange("o (g p t) -> p (o g) t", p=P, t=4))
        load_att(nc.sync, 3, 0, GA)
        load_x(1)
        for g in range(GX):
            load_words(csw, cs_w_words, g)
        load_scales(csw_scl, cs_w_scales)
        load_x(2)
        for g in range(GX, GW):
            load_words(csw, cs_w_words, g)
        load_x(3)
        nc.sync.dma_start(out=bias[:], in_=cs_b.partition_broadcast(P))

        def turned(src, pieces):
            bank = turn.tile([P, 4, P], F32, name="turned")
            words = src[:].bitcast(F32)
            for i in range(len(pieces)):
                nc.tensor.transpose(bank[:, i, :], words[:, pieces[i]], ident[:])
            return bank

        def every_second(g0, n):
            return [slice(256 * g + u, 256 * (g + 1), 2) for g in range(g0, g0 + n) for u in range(2)]

        def side_by_side(g0, n):
            return [slice(128 * i, 128 * (i + 1)) for i in range(2 * g0, 2 * (g0 + n))]

        def emptied(bank, grp, g0, n):
            nc.scalar.copy(
                out=grp[:, g0 : g0 + n, :, :].bitcast(F32),
                in_=bank[:, 0 : 2 * n, :].rearrange("p (g u) r -> p g r u", u=2),
            )

        def quantize(cod, scl, grp, g0, n):
            nc.vector.quantize_mx(
                out=cod[:, g0 : g0 + n, :].rearrange("p g r -> p (g r)").bitcast(FP8X4),
                scales=scl[:, g0 : g0 + n, :].rearrange("p g r -> p (g r)"),
                in_=grp[:, g0 : g0 + n, :, :].rearrange("p g r t -> p (g r t)"),
            )

        def mx(bank, cod, scl, g, tile, tile_scl, gw, n, first, last):
            nc.tensor.matmul_mx(
                out=bank[:],
                lhsT=cod[:, g, :].bitcast(FP8X4),
                lhsT_scale=scl[:, g, :],
                rhs=tile[:, gw, 2 * BANK * n : 2 * BANK * (n + 1)].bitcast(FP4X4),
                rhs_scale=tile_scl[:, gw, BANK * n : BANK * (n + 1)],
                start=first,
                stop=last,
            )

        def sum_banks(count):
            banks = []
            for n in range(count):
                bank = sums.tile([P, BANK], F32, name="sum")
                banks.append(bank)
            return banks

        def x_widen(m, h):
            cols = slice(1024 * h, 1024 * (h + 1))
            COPYX = nc.vector.tensor_copy if m < 2 else nc.scalar.copy
            COPYX(out=xv[m][:, cols], in_=xb[m][:, cols].bitcast(FP8))

        def x_order(m, h):
            cols = slice(1024 * h, 1024 * (h + 1))
            nc.vector.tensor_copy(
                out=xo[m][:, cols].bitcast(F32).rearrange("r (g u p) -> r g u p", u=2, p=P),
                in_=xv[m][:, cols].bitcast(F32).rearrange("r (g p u) -> r g u p", u=2, p=P),
            )

        def x_scaled(bank, m, h, i):
            g = 2 * h + i
            nc.vector.tensor_tensor(
                out=w_grp[m][:, g, :, :].rearrange("p r (u e) -> p r u e", u=2),
                in0=bank[:, 2 * i : 2 * i + 2, :].bitcast(BF16).rearrange("p u (r e) -> p r u e", e=2),
                in1=x_scl[:, g, :].rearrange("p (o u e) -> p o u e", o=1, u=2).to_broadcast([P, P, 2, 2]),
                op=MULT,
            )

        def z_round(bank, m, n):
            nc.scalar.copy(
                out=zo[m][:, BANK * n : BANK * (n + 1)].rearrange("r (u p e) -> r u p e", u=2, e=2),
                in_=bank[:].rearrange("r (p u e) -> r u p e", u=2, e=2),
            )

        def z_keep(bank, m, n):
            nc.scalar.copy(out=zf[m][:, BANK * n : BANK * (n + 1)], in_=bank[:])


        def a_stage(m, cuts):
            for g0, n in cuts:
                bank = turned(att[m], every_second(g0, n))
                emptied(bank, a_grp[m], g0, n)

        def a_quant(m, cuts):
            for g0, n in cuts:
                quantize(a_cod[m], a_scl[m], a_grp[m], g0, n)

        FIRST = [(0, 1), (1, 2)]
        CUTS = [(0, 2), (2, 1)]
        a_stage(0, FIRST)
        a_quant(0, FIRST)
        a_stage(1, CUTS)
        a_quant(1, CUTS)

        for step in range(STEPS):
            a, x, z, l = step + 2, step - 2, step - 1, step - TILES
            xn = {0: [(0, 0), (0, 1)], 1: [(1, 0), (1, 1)], 2: [], 3: [(2, 0), (2, 1)], 4: [(3, 0), (3, 1)]}.get(step, [])
            if step < TILES:
                zbanks = sum_banks(NZ)
                for g in range(GA):
                    for n in range(NZ):
                        mx(zbanks[n], a_cod[step], a_scl[step], g, dic, dic_scl, g, n, g == 0, g == GA - 1)
                for n in range(NZ):
                    z_round(zbanks[n], step, n)
                nc.vector.tensor_copy(out=zf[step][:, 0:BANK], in_=zbanks[0][:])
            elif l < TILES - 1:
                lbanks = sum_banks(NL)
                for g in range(GX):
                    for n in range(NL):
                        mx(lbanks[n], w_cod[l], w_scl[l], g, csw, csw_scl, g, n, g == 0, False)
                for n in range(NL):
                    for g in range(GX, GW):
                        mx(lbanks[n], w_cod[l], w_scl[l], g, csw, csw_scl, g, n, False, g == GW - 1)
            else:
                lbanks = sum_banks(NL)
                for n in range(NL):
                    for g in range(GW):
                        mx(lbanks[n], w_cod[l], w_scl[l], g, csw, csw_scl, g, n, g == 0, g == GW - 1)
            for m, h in xn:
                x_widen(m, h)
            if a < TILES:
                a_stage(a, CUTS)
            if 0 <= x < TILES:
                xbanks = [turned(xo[x], side_by_side(2 * h, 2)) for h in range(2)]
            if 0 <= z < TILES:
                bank = turned(zo[z], side_by_side(0, 2))
            if step < TILES:
                z_keep(zbanks[1], step, 1)
                nc.sync.dma_start(out=out_1[rows(step), :], in_=zf[step][:])
            if 0 <= z < TILES:
                emptied(bank, w_grp[z], GX, GZ)
            for m, h in xn:
                x_order(m, h)
            if a < TILES:
                a_quant(a, CUTS)
            if step >= TILES:
                for n in range(NL):
                    parts = 2 if step == STEPS - 1 and n == NL - 1 else 1
                    for i in range(parts):
                        w = BANK // parts
                        cols = slice(BANK * n + w * i, BANK * n + w * (i + 1))
                        nc.vector.tensor_tensor(out=lo[l][:, cols], in0=lbanks[n][:, w * i : w * (i + 1)], in1=bias[:, cols], op=ADD)
                        nc.sync.dma_start(out=out_0[rows(l), cols], in_=lo[l][:, cols])
            if 0 <= x < TILES:
                for h in range(2):
                    for i in range(2):
                        x_scaled(xbanks[h], x, h, i)
                quantize(w_cod[x], w_scl[x], w_grp[x], 0, GX)
            if 0 <= z < TILES:
                quantize(w_cod[z], w_scl[z], w_grp[z], GX, GZ)
